import numpy as np
import ml_dtypes


def mxq(x, axis, fmt="e4m3"):
    dtype, down = {"e4m3": (ml_dtypes.float8_e4m3fn, 7), "e5m2": (ml_dtypes.float8_e5m2, 14)}[fmt]
    v = np.moveaxis(np.asarray(x, np.float32).astype(ml_dtypes.bfloat16).astype(np.float64), axis, -1)
    blocks = v.reshape(v.shape[:-1] + (-1, 32))
    amax = np.abs(blocks).max(-1, keepdims=True)
    byte = np.maximum(np.where(amax > 0, np.frexp(amax)[1] - 1 + 127, 0) - down, 1)
    scale = np.exp2(byte - 127.0)
    codes = (blocks / scale).astype(np.float32).astype(dtype).astype(np.float64)
    return np.moveaxis((codes * scale).reshape(v.shape), -1, axis)


WIDE = False


def mx_kscale(k):
    if not WIDE:
        return np.ones(k)
    levels = np.array([10, -10, 5, -5, 0])
    a = np.random.permutation(np.resize(levels, k // 512 * 4)).reshape(k // 512, 4)
    idx = np.arange(k)
    return np.exp2(a[idx // 512, idx % 128 // 32])


BF16 = ml_dtypes.bfloat16


def bf(x):
    return np.asarray(x, np.float32).astype(BF16)


def f64(x):
    return np.asarray(x).astype(np.float64)


E2M1 = np.array([0.0, 0.5, 1.0, 1.5, 2.0, 3.0, 4.0, 6.0, -0.0, -0.5, -1.0, -1.5, -2.0, -3.0, -4.0, -6.0])


def pack_weight(w, fmt):
    k, n = w.shape
    w = f64(bf(w)).reshape(k // 32, 32, n)
    amax = np.abs(w).max(1)
    if fmt == "e4m3":
        byte = np.frexp(amax)[1] - 1 + 127 - 7
    else:
        mant, ex = np.frexp(amax / 6.0)
        byte = np.where(mant > 0.5, ex, ex - 1) + 127
    byte = np.clip(np.where(amax > 0, byte, 1), 1, 254)
    scaled = (w * np.exp2(127.0 - byte)[:, None, :]).reshape(k, n).astype(np.float32)
    by_word = np.ascontiguousarray(scaled.reshape(k // 512, 128, 4, n).transpose(0, 1, 3, 2))
    if fmt == "e4m3":
        words = by_word.astype(ml_dtypes.float8_e4m3fn).view(np.uint8)
    else:
        c = by_word.astype(ml_dtypes.float4_e2m1fn).view(np.uint8) & 0xF
        words = c[..., 0::2] | (c[..., 1::2] << 4)
    return np.ascontiguousarray(words), np.ascontiguousarray(byte.astype(np.uint8).reshape(k // 512, 16, n))


def unpack_weight(words, scales, fmt):
    g, p, n, _ = words.shape
    if fmt == "e4m3":
        vals = np.ascontiguousarray(words).view(ml_dtypes.float8_e4m3fn).astype(np.float64)
    else:
        nib = np.empty((g, p, n, 4), np.uint8)
        nib[..., 0::2] = words & 0xF
        nib[..., 1::2] = words >> 4
        vals = E2M1[nib]
    vals = vals * np.repeat(np.exp2(scales.astype(np.float64) - 127.0), 8, axis=1)[..., None]
    return vals.transpose(0, 1, 3, 2).reshape(g * 512, n)

def pack4(w):
    words, scales = pack_weight(w, "e2m1")
    return words.reshape(words.shape[0], 128, -1), scales


def unpack4(words, scales):
    return unpack_weight(words.reshape(words.shape[0], 128, -1, 2), scales, "e2m1")


B, T, C, E, DV, R, G, BLK = 1, 1024, 1024, 1024, 1024, 16, 16, 512
BASE = 1e4


def rope(x):
    inv_freq = 1.0 / (BASE ** (f64(np.arange(0, R, 2)) / R))
    ang = f64(np.arange(T))[:, None] * inv_freq[None, :]
    ang = np.repeat(ang, 2, axis=-1)
    cos, sin = np.cos(ang), np.sin(ang)
    xl, xr = x[..., :R], x[..., R:]
    p = xl.reshape(xl.shape[:-1] + (R // 2, 2))
    rot = np.stack((-p[..., 1], p[..., 0]), axis=-1).reshape(xl.shape)
    return np.concatenate([xl * cos + rot * sin, xr], axis=-1)


def setup_inputs():
    s = mx_kscale(C)
    Q_in = bf(np.random.standard_normal((B, T, C)) * s)
    wq_words, wq_scales = pack4(np.random.standard_normal((C, E)) * 0.25 / np.sqrt(C) / s[:, None])
    wk_words, wk_scales = pack4(np.random.standard_normal((C, E)) * 0.25 / np.sqrt(C) / s[:, None])
    return {"Q_in": Q_in,
            "W_Q_words": wq_words, "W_Q_scales": wq_scales,
            "W_K_words": wk_words, "W_K_scales": wk_scales}


def reference(Q_in, W_Q_words, W_Q_scales, W_K_words, W_K_scales):
    xq = mxq(f64(Q_in), 2, "e4m3")
    q = rope(xq @ unpack4(W_Q_words, W_Q_scales))
    k = rope(xq @ unpack4(W_K_words, W_K_scales))
    return q, k

@@ -1,0 +1,215 @@
+import math
+from contextlib import ExitStack
+
+import concourse.mybir as mybir
+from concourse.masks import make_identity
+
+F32 = mybir.dt.float32
+BF16 = mybir.dt.bfloat16
+I32 = mybir.dt.int32
+U32 = mybir.dt.uint32
+U8 = mybir.dt.uint8
+FP8X4 = mybir.dt.float8_e4m3fn_x4
+FP4X4 = mybir.dt.float4_e2m1fn_x4
+ALU = mybir.AluOpType
+
+P = 128
+PACK = 4
+K_PASS = P * PACK
+PASS_WORDS = K_PASS // 2
+TOKENS = 1024
+CHANNELS = 1024
+OUT_COLS = 1024
+PASSES = CHANNELS // K_PASS
+TOKEN_TILES = TOKENS // P
+N_TILE = 512
+COL_TILES = OUT_COLS // N_TILE
+WEIGHTS = 2
+ROPE_COLS = 16
+ROPE_PAIRS = ROPE_COLS // 2
+ROPE_BASE = 1e4
+ROUND_TO_INTEGER = 1.5 * 2.0**23
+
+FLOPS = 2 * TOKENS * CHANNELS * OUT_COLS * WEIGHTS
+
+
+def tile_wqkv_pa_kernel(
+    tc, Q_in, W_Q_words, W_Q_scales, W_K_words, W_K_scales, out_0, out_1
+):
+    nc = tc.nc
+    x_dram = Q_in.rearrange("b (p i) c -> (b p) i c", i=TOKEN_TILES)
+    out_dram = [
+        out.rearrange("b (p i) e -> (b p) i e", i=TOKEN_TILES) for out in (out_0, out_1)
+    ]
+    words_dram = [W_Q_words, W_K_words]
+    scales_dram = [W_Q_scales, W_K_scales]
+
+    with ExitStack() as ctx:
+        ctx.enter_context(tc.manual_schedule())
+        keep = ctx.enter_context(tc.tile_pool(name="keep", bufs=1))
+        stage = ctx.enter_context(tc.tile_pool(name="stage", bufs=3))
+        results = ctx.enter_context(tc.tile_pool(name="results", bufs=4))
+        flipped = ctx.enter_context(tc.psum_pool(name="flipped", bufs=2))
+        sums = ctx.enter_context(tc.psum_pool(name="sums", bufs=6))
+
+        x_tiles = []
+
+        def load_x(count):
+            first = len(x_tiles)
+            x_group = keep.tile([P, count, CHANNELS], BF16, name="x%d" % first)
+            nc.sync.dma_start(out=x_group[:], in_=x_dram[:, first : first + count, :])
+            x_tiles.extend([x_group[:, j, :] for j in range(count)])
+
+        w_words = [
+            keep.tile([P, PASSES, 2 * OUT_COLS], U8, name="w_words%d" % w, align_bytes=64)
+            for w in range(WEIGHTS)
+        ]
+        w_scales = keep.tile([P, WEIGHTS, PASSES, OUT_COLS], U8, name="w_scales", align_bytes=64)
+        nc.vector.memset(w_scales[:].rearrange("p w g n -> p (w g n)").bitcast(I32), 0)
+
+        def load_weight(w):
+            nc.sync.dma_start(
+                out=w_words[w][:].bitcast(I32),
+                in_=words_dram[w].bitcast(I32).rearrange("g p b -> p g b"),
+            )
+            for r in range(4):
+                nc.sync.dma_start(
+                    out=w_scales[r:P:32, w, :, :].bitcast(I32),
+                    in_=scales_dram[w].bitcast(I32)[:, r:16:4, :].rearrange("g q n -> q g n"),
+                )
+
+        load_x(1)
+        load_x(1)
+        load_weight(0)
+        load_weight(1)
+        while len(x_tiles) < TOKEN_TILES:
+            load_x(len(x_tiles))
+
+        position = keep.tile([P, TOKEN_TILES], F32, name="position")
+        nc.gpsimd.iota(
+            position[:],
+            pattern=[[1, TOKEN_TILES]],
+            base=0,
+            channel_multiplier=TOKEN_TILES,
+            allow_small_or_imprecise_dtypes=True,
+        )
+        identity = keep.tile([P, P], F32, name="identity")
+        make_identity(nc, identity[:])
+
+        turns = keep.tile([P, TOKEN_TILES, 2, ROPE_PAIRS], F32, name="turns")
+        for j in range(ROPE_PAIRS):
+            nc.vector.tensor_scalar(
+                out=turns[:, :, 1, j],
+                in0=position[:],
+                scalar1=1.0 / (2.0 * math.pi * ROPE_BASE ** (2.0 * j / ROPE_COLS)),
+                scalar2=None,
+                op0=ALU.mult,
+            )
+        nc.vector.tensor_scalar(
+            out=turns[:, :, 0, :], in0=turns[:, :, 1, :], scalar1=0.25, scalar2=None, op0=ALU.add
+        )
+        whole = keep.tile([P, TOKEN_TILES, 2, ROPE_PAIRS], F32, name="whole")
+        nc.vector.tensor_scalar(
+            out=whole[:],
+            in0=turns[:],
+            scalar1=ROUND_TO_INTEGER,
+            scalar2=ROUND_TO_INTEGER,
+            op0=ALU.add,
+            op1=ALU.subtract,
+        )
+        part = keep.tile([P, TOKEN_TILES, 2, ROPE_PAIRS], F32, name="part")
+        nc.vector.tensor_tensor(out=part[:], in0=turns[:], in1=whole[:], op=ALU.subtract)
+        cos_sin = keep.tile([P, TOKEN_TILES, 2, ROPE_COLS], F32, name="cos_sin")
+        nc.scalar.activation(
+            out=cos_sin[:].rearrange("p i h (j e) -> p (i h j) e", e=2),
+            in_=part[:]
+            .rearrange("p i h j -> p (i h j)")
+            .unsqueeze(2)
+            .to_broadcast([P, TOKEN_TILES * 2 * ROPE_PAIRS, 2]),
+            func=mybir.ActivationFunctionType.Sin,
+            scale=2.0 * math.pi,
+        )
+
+        x_codes = {}
+        x_scales = {}
+
+        def quantise_tile(i):
+            x_words = x_tiles[i].bitcast(F32)
+            turned = flipped.tile([P, PASSES, 2, P], F32, name="turned")
+            for g in range(PASSES):
+                for u in range(2):
+                    nc.tensor.transpose(
+                        turned[:, g, u, :],
+                        x_words[:, PASS_WORDS * g + u : PASS_WORDS * (g + 1) : 2],
+                        identity[:],
+                    )
+            grouped = stage.tile([P, PASSES, P, PACK], BF16, name="grouped", align_bytes=64)
+            nc.scalar.copy(
+                out=grouped[:].bitcast(F32), in_=turned[:].rearrange("p g u r -> p g r u")
+            )
+            codes = stage.tile([P, PASSES * P], U32, name="codes", align_bytes=64)
+            scales = stage.tile([P, PASSES * P], U8, name="scales", align_bytes=64)
+            nc.vector.quantize_mx(
+                out=codes[:].bitcast(FP8X4),
+                scales=scales[:],
+                in_=grouped[:].rearrange("p g r t -> p (g r t)"),
+            )
+            x_codes[i] = codes
+            x_scales[i] = scales
+
+        def project_tile(i):
+            result = results.tile([P, WEIGHTS, OUT_COLS], F32, name="result")
+            for c in range(COL_TILES):
+                first_col = N_TILE * c
+                cols = slice(first_col, first_col + N_TILE)
+                word_bytes = slice(2 * first_col, 2 * (first_col + N_TILE))
+                for w in range(WEIGHTS):
+                    acc = sums.tile([P, N_TILE], F32, name="acc")
+                    for g in range(PASSES):
+                        tokens = slice(P * g, P * (g + 1))
+                        nc.tensor.matmul_mx(
+                            out=acc[:],
+                            lhsT=x_codes[i][:, tokens].bitcast(FP8X4),
+                            lhsT_scale=x_scales[i][:, tokens],
+                            rhs=w_words[w][:, g, word_bytes].bitcast(FP4X4),
+                            rhs_scale=w_scales[:, w, g, cols],
+                            start=(g == 0),
+                            stop=(g == PASSES - 1),
+                        )
+                    if c == 0:
+                        nc.vector.tensor_copy(out=result[:, w, cols], in_=acc[:])
+                    else:
+                        nc.scalar.copy(out=result[:, w, cols], in_=acc[:])
+                if c == 0:
+                    rope(i, result)
+            for w in range(WEIGHTS):
+                nc.sync.dma_start(out=out_dram[w][:, i, :], in_=result[:, w, :])
+
+        def rope(i, result):
+            head = result[:, :, 0:ROPE_COLS]
+            shape = [P, 2, WEIGHTS, ROPE_COLS]
+            products = stage.tile(shape, F32, name="products")
+            nc.vector.tensor_tensor(
+                out=products[:],
+                in0=head.unsqueeze(1).to_broadcast(shape),
+                in1=cos_sin[:, i].unsqueeze(2).to_broadcast(shape),
+                op=ALU.mult,
+            )
+            nc.vector.tensor_tensor(
+                out=head[:, :, 0:ROPE_COLS:2],
+                in0=products[:, 0, :, 0:ROPE_COLS:2],
+                in1=products[:, 1, :, 1:ROPE_COLS:2],
+                op=ALU.subtract,
+            )
+            nc.vector.tensor_tensor(
+                out=head[:, :, 1:ROPE_COLS:2],
+                in0=products[:, 0, :, 1:ROPE_COLS:2],
+                in1=products[:, 1, :, 0:ROPE_COLS:2],
+                op=ALU.add,
+            )
+
+        quantise_tile(0)
+        for i in range(TOKEN_TILES):
+            if i + 1 < TOKEN_TILES:
+                quantise_tile(i + 1)
+            project_tile(i)

@@ -64,8 +64,12 @@ def tile_wqkv_pa_kernel(
             keep.tile([P, PASSES, 2 * OUT_COLS], U8, name="w_words%d" % w, align_bytes=64)
             for w in range(WEIGHTS)
         ]
-        w_scales = keep.tile([P, WEIGHTS, PASSES, OUT_COLS], U8, name="w_scales", align_bytes=64)
-        nc.vector.memset(w_scales[:].rearrange("p w g n -> p (w g n)").bitcast(I32), 0)
+        w_scales = [
+            keep.tile([P, PASSES, OUT_COLS], U8, name="w_scales%d" % w, align_bytes=64)
+            for w in range(WEIGHTS)
+        ]
+        for w in range(WEIGHTS):
+            nc.vector.memset(w_scales[w][:].rearrange("p g n -> p (g n)").bitcast(I32), 0)
 
         def load_weight(w):
             nc.sync.dma_start(
@@ -74,7 +78,7 @@ def tile_wqkv_pa_kernel(
             )
             for r in range(4):
                 nc.sync.dma_start(
-                    out=w_scales[r:P:32, w, :, :].bitcast(I32),
+                    out=w_scales[w][r:P:32, :, :].bitcast(I32),
                     in_=scales_dram[w].bitcast(I32)[:, r:16:4, :].rearrange("g q n -> q g n"),
                 )
 
@@ -130,10 +134,11 @@ def tile_wqkv_pa_kernel(
             scale=2.0 * math.pi,
         )
 
+        x_grouped = {}
         x_codes = {}
         x_scales = {}
 
-        def quantise_tile(i):
+        def turn_tile(i):
             x_words = x_tiles[i].bitcast(F32)
             turned = flipped.tile([P, PASSES, 2, P], F32, name="turned")
             for g in range(PASSES):
@@ -147,43 +152,45 @@ def tile_wqkv_pa_kernel(
             nc.scalar.copy(
                 out=grouped[:].bitcast(F32), in_=turned[:].rearrange("p g u r -> p g r u")
             )
+            x_grouped[i] = grouped
+
+        def quantise_tile(i):
             codes = stage.tile([P, PASSES * P], U32, name="codes", align_bytes=64)
             scales = stage.tile([P, PASSES * P], U8, name="scales", align_bytes=64)
             nc.vector.quantize_mx(
                 out=codes[:].bitcast(FP8X4),
                 scales=scales[:],
-                in_=grouped[:].rearrange("p g r t -> p (g r t)"),
+                in_=x_grouped[i][:].rearrange("p g r t -> p (g r t)"),
             )
             x_codes[i] = codes
             x_scales[i] = scales
 
-        def project_tile(i):
-            result = results.tile([P, WEIGHTS, OUT_COLS], F32, name="result")
-            for c in range(COL_TILES):
-                first_col = N_TILE * c
-                cols = slice(first_col, first_col + N_TILE)
-                word_bytes = slice(2 * first_col, 2 * (first_col + N_TILE))
-                for w in range(WEIGHTS):
-                    acc = sums.tile([P, N_TILE], F32, name="acc")
-                    for g in range(PASSES):
-                        tokens = slice(P * g, P * (g + 1))
-                        nc.tensor.matmul_mx(
-                            out=acc[:],
-                            lhsT=x_codes[i][:, tokens].bitcast(FP8X4),
-                            lhsT_scale=x_scales[i][:, tokens],
-                            rhs=w_words[w][:, g, word_bytes].bitcast(FP4X4),
-                            rhs_scale=w_scales[:, w, g, cols],
-                            start=(g == 0),
-                            stop=(g == PASSES - 1),
-                        )
-                    if c == 0:
-                        nc.vector.tensor_copy(out=result[:, w, cols], in_=acc[:])
-                    else:
-                        nc.scalar.copy(out=result[:, w, cols], in_=acc[:])
-                if c == 0:
-                    rope(i, result)
+        def project(i, c, copy_out):
+            first_col = N_TILE * c
+            cols = slice(first_col, first_col + N_TILE)
+            word_bytes = slice(2 * first_col, 2 * (first_col + N_TILE))
+            result = results.tile([P, WEIGHTS, N_TILE], F32, name="result%d" % c)
             for w in range(WEIGHTS):
-                nc.sync.dma_start(out=out_dram[w][:, i, :], in_=result[:, w, :])
+                acc = sums.tile([P, N_TILE], F32, name="acc")
+                for g in range(PASSES):
+                    tokens = slice(P * g, P * (g + 1))
+                    nc.tensor.matmul_mx(
+                        out=acc[:],
+                        lhsT=x_codes[i][:, tokens].bitcast(FP8X4),
+                        lhsT_scale=x_scales[i][:, tokens],
+                        rhs=w_words[w][:, g, word_bytes].bitcast(FP4X4),
+                        rhs_scale=w_scales[w][:, g, cols],
+                        start=(g == 0),
+                        stop=(g == PASSES - 1),
+                    )
+                copy_out(out=result[:, w, :], in_=acc[:])
+            return result
+
+        def store(i, c, result):
+            for w in range(WEIGHTS):
+                nc.sync.dma_start(
+                    out=out_dram[w][:, i, N_TILE * c : N_TILE * (c + 1)], in_=result[:, w, :]
+                )
 
         def rope(i, result):
             head = result[:, :, 0:ROPE_COLS]
@@ -208,8 +215,15 @@ def tile_wqkv_pa_kernel(
                 op=ALU.add,
             )
 
+        turn_tile(0)
         quantise_tile(0)
         for i in range(TOKEN_TILES):
             if i + 1 < TOKEN_TILES:
+                turn_tile(i + 1)
+            low = project(i, 0, nc.vector.tensor_copy)
+            if i + 1 < TOKEN_TILES:
                 quantise_tile(i + 1)
-            project_tile(i)
+            rope(i, low)
+            store(i, 0, low)
+            high = project(i, 1, nc.scalar.copy)
+            store(i, 1, high)

@@ -29,6 +29,7 @@ ROPE_COLS = 16
 ROPE_PAIRS = ROPE_COLS // 2
 ROPE_BASE = 1e4
 ROUND_TO_INTEGER = 1.5 * 2.0**23
+RUN = 2
 
 FLOPS = 2 * TOKENS * CHANNELS * OUT_COLS * WEIGHTS
 
@@ -49,7 +50,8 @@ def tile_wqkv_pa_kernel(
         keep = ctx.enter_context(tc.tile_pool(name="keep", bufs=1))
         stage = ctx.enter_context(tc.tile_pool(name="stage", bufs=3))
         results = ctx.enter_context(tc.tile_pool(name="results", bufs=4))
-        flipped = ctx.enter_context(tc.psum_pool(name="flipped", bufs=2))
+        ordered = ctx.enter_context(tc.tile_pool(name="ordered", bufs=2 * RUN))
+        flipped = ctx.enter_context(tc.psum_pool(name="flipped", bufs=RUN))
         sums = ctx.enter_context(tc.psum_pool(name="sums", bufs=6))
 
         x_tiles = []
@@ -134,20 +136,24 @@ def tile_wqkv_pa_kernel(
             scale=2.0 * math.pi,
         )
 
+        x_sorted = {}
         x_grouped = {}
         x_codes = {}
         x_scales = {}
 
+        def sort_tile(i):
+            words = ordered.tile([P, PASSES, 2, P], F32, name="words")
+            nc.vector.tensor_copy(
+                out=words[:],
+                in_=x_tiles[i].bitcast(F32).rearrange("p (g q u) -> p g u q", g=PASSES, u=2),
+            )
+            x_sorted[i] = words
+
         def turn_tile(i):
-            x_words = x_tiles[i].bitcast(F32)
             turned = flipped.tile([P, PASSES, 2, P], F32, name="turned")
             for g in range(PASSES):
                 for u in range(2):
-                    nc.tensor.transpose(
-                        turned[:, g, u, :],
-                        x_words[:, PASS_WORDS * g + u : PASS_WORDS * (g + 1) : 2],
-                        identity[:],
-                    )
+                    nc.tensor.transpose(turned[:, g, u, :], x_sorted[i][:, g, u, :], identity[:])
             grouped = stage.tile([P, PASSES, P, PACK], BF16, name="grouped", align_bytes=64)
             nc.scalar.copy(
                 out=grouped[:].bitcast(F32), in_=turned[:].rearrange("p g u r -> p g r u")
@@ -215,14 +221,24 @@ def tile_wqkv_pa_kernel(
                 op=ALU.add,
             )
 
-        turn_tile(0)
+        def tiles_from(first):
+            return range(first, min(first + RUN, TOKEN_TILES))
+
+        for t in tiles_from(0):
+            sort_tile(t)
+        for t in tiles_from(0):
+            turn_tile(t)
         quantise_tile(0)
         for i in range(TOKEN_TILES):
-            if i + 1 < TOKEN_TILES:
-                turn_tile(i + 1)
-            low = project(i, 0, nc.vector.tensor_copy)
+            if i % RUN == RUN - 1:
+                for t in tiles_from(i + 1):
+                    turn_tile(t)
             if i + 1 < TOKEN_TILES:
                 quantise_tile(i + 1)
+            if i % RUN == 0:
+                for t in tiles_from(i + RUN):
+                    sort_tile(t)
+            low = project(i, 0, nc.vector.tensor_copy)
             rope(i, low)
             store(i, 0, low)
             high = project(i, 1, nc.scalar.copy)

@@ -30,6 +30,8 @@ ROPE_PAIRS = ROPE_COLS // 2
 ROPE_BASE = 1e4
 ROUND_TO_INTEGER = 1.5 * 2.0**23
 RUN = 2
+IDLE_WHILE_LOADING = 5
+IDLE_WHILE_QUANTISING = 3
 
 FLOPS = 2 * TOKENS * CHANNELS * OUT_COLS * WEIGHTS
 
@@ -53,6 +55,18 @@ def tile_wqkv_pa_kernel(
         ordered = ctx.enter_context(tc.tile_pool(name="ordered", bufs=2 * RUN))
         flipped = ctx.enter_context(tc.psum_pool(name="flipped", bufs=RUN))
         sums = ctx.enter_context(tc.psum_pool(name="sums", bufs=6))
+
+        zeros = keep.tile([P, N_TILE], BF16, name="zeros")
+        nc.vector.memset(zeros[:].bitcast(I32), 0)
+
+        def idle_matmuls(count):
+            unread = sums.tile([P, N_TILE], F32, name="acc")
+            for n in range(count):
+                nc.tensor.matmul(
+                    out=unread[:], lhsT=zeros[:, 0:P], rhs=zeros[:], start=True, stop=True
+                )
+
+        idle_matmuls(IDLE_WHILE_LOADING)
 
         x_tiles = []
 
@@ -228,6 +242,7 @@ def tile_wqkv_pa_kernel(
             sort_tile(t)
         for t in tiles_from(0):
             turn_tile(t)
+        idle_matmuls(IDLE_WHILE_QUANTISING)
         quantise_tile(0)
         for i in range(TOKEN_TILES):
             if i % RUN == RUN - 1:

@@ -30,8 +30,6 @@ ROPE_PAIRS = ROPE_COLS // 2
 ROPE_BASE = 1e4
 ROUND_TO_INTEGER = 1.5 * 2.0**23
 RUN = 2
-IDLE_WHILE_LOADING = 5
-IDLE_WHILE_QUANTISING = 3
 
 FLOPS = 2 * TOKENS * CHANNELS * OUT_COLS * WEIGHTS
 
@@ -55,18 +53,6 @@ def tile_wqkv_pa_kernel(
         ordered = ctx.enter_context(tc.tile_pool(name="ordered", bufs=2 * RUN))
         flipped = ctx.enter_context(tc.psum_pool(name="flipped", bufs=RUN))
         sums = ctx.enter_context(tc.psum_pool(name="sums", bufs=6))
-
-        zeros = keep.tile([P, N_TILE], BF16, name="zeros")
-        nc.vector.memset(zeros[:].bitcast(I32), 0)
-
-        def idle_matmuls(count):
-            unread = sums.tile([P, N_TILE], F32, name="acc")
-            for n in range(count):
-                nc.tensor.matmul(
-                    out=unread[:], lhsT=zeros[:, 0:P], rhs=zeros[:], start=True, stop=True
-                )
-
-        idle_matmuls(IDLE_WHILE_LOADING)
 
         x_tiles = []
 
@@ -185,11 +171,10 @@ def tile_wqkv_pa_kernel(
             x_codes[i] = codes
             x_scales[i] = scales
 
-        def project(i, c, copy_out):
+        def project(i, c, copy_out, result):
             first_col = N_TILE * c
             cols = slice(first_col, first_col + N_TILE)
             word_bytes = slice(2 * first_col, 2 * (first_col + N_TILE))
-            result = results.tile([P, WEIGHTS, N_TILE], F32, name="result%d" % c)
             for w in range(WEIGHTS):
                 acc = sums.tile([P, N_TILE], F32, name="acc")
                 for g in range(PASSES):
@@ -203,37 +188,30 @@ def tile_wqkv_pa_kernel(
                         start=(g == 0),
                         stop=(g == PASSES - 1),
                     )
-                copy_out(out=result[:, w, :], in_=acc[:])
-            return result
-
-        def store(i, c, result):
-            for w in range(WEIGHTS):
-                nc.sync.dma_start(
-                    out=out_dram[w][:, i, N_TILE * c : N_TILE * (c + 1)], in_=result[:, w, :]
-                )
+                copy_out(out=result[w][:, cols], in_=acc[:])
 
         def rope(i, result):
-            head = result[:, :, 0:ROPE_COLS]
-            shape = [P, 2, WEIGHTS, ROPE_COLS]
-            products = stage.tile(shape, F32, name="products")
-            nc.vector.tensor_tensor(
-                out=products[:],
-                in0=head.unsqueeze(1).to_broadcast(shape),
-                in1=cos_sin[:, i].unsqueeze(2).to_broadcast(shape),
-                op=ALU.mult,
-            )
-            nc.vector.tensor_tensor(
-                out=head[:, :, 0:ROPE_COLS:2],
-                in0=products[:, 0, :, 0:ROPE_COLS:2],
-                in1=products[:, 1, :, 1:ROPE_COLS:2],
-                op=ALU.subtract,
-            )
-            nc.vector.tensor_tensor(
-                out=head[:, :, 1:ROPE_COLS:2],
-                in0=products[:, 0, :, 1:ROPE_COLS:2],
-                in1=products[:, 1, :, 0:ROPE_COLS:2],
-                op=ALU.add,
-            )
+            products = stage.tile([P, WEIGHTS, 2, ROPE_COLS], F32, name="products")
+            for w in range(WEIGHTS):
+                nc.vector.tensor_tensor(
+                    out=products[:, w],
+                    in0=result[w][:, 0:ROPE_COLS].unsqueeze(1).to_broadcast([P, 2, ROPE_COLS]),
+                    in1=cos_sin[:, i],
+                    op=ALU.mult,
+                )
+            for w in range(WEIGHTS):
+                nc.vector.tensor_tensor(
+                    out=result[w][:, 0:ROPE_COLS:2],
+                    in0=products[:, w, 0, 0:ROPE_COLS:2],
+                    in1=products[:, w, 1, 1:ROPE_COLS:2],
+                    op=ALU.subtract,
+                )
+                nc.vector.tensor_tensor(
+                    out=result[w][:, 1:ROPE_COLS:2],
+                    in0=products[:, w, 0, 1:ROPE_COLS:2],
+                    in1=products[:, w, 1, 0:ROPE_COLS:2],
+                    op=ALU.add,
+                )
 
         def tiles_from(first):
             return range(first, min(first + RUN, TOKEN_TILES))
@@ -242,7 +220,6 @@ def tile_wqkv_pa_kernel(
             sort_tile(t)
         for t in tiles_from(0):
             turn_tile(t)
-        idle_matmuls(IDLE_WHILE_QUANTISING)
         quantise_tile(0)
         for i in range(TOKEN_TILES):
             if i % RUN == RUN - 1:
@@ -253,8 +230,11 @@ def tile_wqkv_pa_kernel(
             if i % RUN == 0:
                 for t in tiles_from(i + RUN):
                     sort_tile(t)
-            low = project(i, 0, nc.vector.tensor_copy)
-            rope(i, low)
-            store(i, 0, low)
-            high = project(i, 1, nc.scalar.copy)
-            store(i, 1, high)
+            result = [
+                results.tile([P, OUT_COLS], F32, name="result%d" % w) for w in range(WEIGHTS)
+            ]
+            project(i, 0, nc.vector.tensor_copy, result)
+            rope(i, result)
+            project(i, 1, nc.scalar.copy, result)
+            for w in range(WEIGHTS):
+                nc.sync.dma_start(out=out_dram[w][:, i, :], in_=result[w][:])

@@ -102,20 +102,41 @@ def tile_wqkv_pa_kernel(
         identity = keep.tile([P, P], F32, name="identity")
         make_identity(nc, identity[:])
 
+        warm = keep.tile([P, 1], F32, name="warm")
+        nc.scalar.activation(
+            out=warm[:], in_=position[:, 0:1], func=mybir.ActivationFunctionType.Sin, scale=0.0
+        )
+
         turns = keep.tile([P, TOKEN_TILES, 2, ROPE_PAIRS], F32, name="turns")
-        for j in range(ROPE_PAIRS):
-            nc.vector.tensor_scalar(
-                out=turns[:, :, 1, j],
-                in0=position[:],
-                scalar1=1.0 / (2.0 * math.pi * ROPE_BASE ** (2.0 * j / ROPE_COLS)),
-                scalar2=None,
+        nc.gpsimd.tensor_scalar(
+            out=turns[:, :, 1, 0],
+            in0=position[:],
+            scalar1=1.0 / (2.0 * math.pi),
+            scalar2=0.0,
+            op0=ALU.mult,
+            op1=ALU.add,
+        )
+        done = 1
+        while done < ROPE_PAIRS:
+            nc.gpsimd.tensor_scalar(
+                out=turns[:, :, 1, done : 2 * done],
+                in0=turns[:, :, 1, 0:done],
+                scalar1=ROPE_BASE ** (-2.0 * done / ROPE_COLS),
+                scalar2=0.0,
                 op0=ALU.mult,
+                op1=ALU.add,
             )
-        nc.vector.tensor_scalar(
-            out=turns[:, :, 0, :], in0=turns[:, :, 1, :], scalar1=0.25, scalar2=None, op0=ALU.add
+            done *= 2
+        nc.gpsimd.tensor_scalar(
+            out=turns[:, :, 0, :],
+            in0=turns[:, :, 1, :],
+            scalar1=1.0,
+            scalar2=0.25,
+            op0=ALU.mult,
+            op1=ALU.add,
         )
         whole = keep.tile([P, TOKEN_TILES, 2, ROPE_PAIRS], F32, name="whole")
-        nc.vector.tensor_scalar(
+        nc.gpsimd.tensor_scalar(
             out=whole[:],
             in0=turns[:],
             scalar1=ROUND_TO_INTEGER,
@@ -124,17 +145,23 @@ def tile_wqkv_pa_kernel(
             op1=ALU.subtract,
         )
         part = keep.tile([P, TOKEN_TILES, 2, ROPE_PAIRS], F32, name="part")
-        nc.vector.tensor_tensor(out=part[:], in0=turns[:], in1=whole[:], op=ALU.subtract)
-        cos_sin = keep.tile([P, TOKEN_TILES, 2, ROPE_COLS], F32, name="cos_sin")
-        nc.scalar.activation(
-            out=cos_sin[:].rearrange("p i h (j e) -> p (i h j) e", e=2),
-            in_=part[:]
-            .rearrange("p i h j -> p (i h j)")
-            .unsqueeze(2)
-            .to_broadcast([P, TOKEN_TILES * 2 * ROPE_PAIRS, 2]),
-            func=mybir.ActivationFunctionType.Sin,
-            scale=2.0 * math.pi,
-        )
+        nc.gpsimd.tensor_tensor(out=part[:], in0=turns[:], in1=whole[:], op=ALU.subtract)
+        rotation = keep.tile([P, TOKEN_TILES, ROPE_PAIRS, 4], F32, name="rotation")
+
+        def make_rotation():
+            nc.scalar.activation(
+                out=rotation[:, :, :, 0:4:3],
+                in_=part[:, :, 0, :].unsqueeze(3).to_broadcast([P, TOKEN_TILES, ROPE_PAIRS, 2]),
+                func=mybir.ActivationFunctionType.Sin,
+                scale=2.0 * math.pi,
+            )
+            for entry, sign in ((1, -1.0), (2, 1.0)):
+                nc.scalar.activation(
+                    out=rotation[:, :, :, entry],
+                    in_=part[:, :, 1, :],
+                    func=mybir.ActivationFunctionType.Sin,
+                    scale=sign * 2.0 * math.pi,
+                )
 
         x_sorted = {}
         x_grouped = {}
@@ -171,47 +198,50 @@ def tile_wqkv_pa_kernel(
             x_codes[i] = codes
             x_scales[i] = scales
 
-        def project(i, c, copy_out, result):
+        def multiply(i, c, w):
             first_col = N_TILE * c
-            cols = slice(first_col, first_col + N_TILE)
-            word_bytes = slice(2 * first_col, 2 * (first_col + N_TILE))
-            for w in range(WEIGHTS):
-                acc = sums.tile([P, N_TILE], F32, name="acc")
-                for g in range(PASSES):
-                    tokens = slice(P * g, P * (g + 1))
-                    nc.tensor.matmul_mx(
-                        out=acc[:],
-                        lhsT=x_codes[i][:, tokens].bitcast(FP8X4),
-                        lhsT_scale=x_scales[i][:, tokens],
-                        rhs=w_words[w][:, g, word_bytes].bitcast(FP4X4),
-                        rhs_scale=w_scales[w][:, g, cols],
-                        start=(g == 0),
-                        stop=(g == PASSES - 1),
-                    )
-                copy_out(out=result[w][:, cols], in_=acc[:])
+            acc = sums.tile([P, N_TILE], F32, name="acc")
+            for g in range(PASSES):
+                tokens = slice(P * g, P * (g + 1))
+                nc.tensor.matmul_mx(
+                    out=acc[:],
+                    lhsT=x_codes[i][:, tokens].bitcast(FP8X4),
+                    lhsT_scale=x_scales[i][:, tokens],
+                    rhs=w_words[w][:, g, 2 * first_col : 2 * (first_col + N_TILE)].bitcast(FP4X4),
+                    rhs_scale=w_scales[w][:, g, first_col : first_col + N_TILE],
+                    start=(g == 0),
+                    stop=(g == PASSES - 1),
+                )
+            return acc
 
-        def rope(i, result):
-            products = stage.tile([P, WEIGHTS, 2, ROPE_COLS], F32, name="products")
+        def project_with_rope(i, result):
+            products = []
             for w in range(WEIGHTS):
+                acc = multiply(i, 0, w)
+                terms = stage.tile([P, ROPE_PAIRS, 2, 2], F32, name="terms%d" % w)
                 nc.vector.tensor_tensor(
-                    out=products[:, w],
-                    in0=result[w][:, 0:ROPE_COLS].unsqueeze(1).to_broadcast([P, 2, ROPE_COLS]),
-                    in1=cos_sin[:, i],
+                    out=terms[:],
+                    in0=acc[:, 0:ROPE_COLS]
+                    .rearrange("p (j c) -> p j c", c=2)
+                    .unsqueeze(2)
+                    .to_broadcast([P, ROPE_PAIRS, 2, 2]),
+                    in1=rotation[:, i].rearrange("p j (r c) -> p j r c", c=2),
                     op=ALU.mult,
                 )
+                nc.vector.tensor_copy(out=result[w][:, ROPE_COLS:N_TILE], in_=acc[:, ROPE_COLS:N_TILE])
+                products.append(terms)
             for w in range(WEIGHTS):
-                nc.vector.tensor_tensor(
-                    out=result[w][:, 0:ROPE_COLS:2],
-                    in0=products[:, w, 0, 0:ROPE_COLS:2],
-                    in1=products[:, w, 1, 1:ROPE_COLS:2],
-                    op=ALU.subtract,
-                )
-                nc.vector.tensor_tensor(
-                    out=result[w][:, 1:ROPE_COLS:2],
-                    in0=products[:, w, 0, 1:ROPE_COLS:2],
-                    in1=products[:, w, 1, 0:ROPE_COLS:2],
+                nc.vector.tensor_reduce(
+                    out=result[w][:, 0:ROPE_COLS],
+                    in_=products[w][:].rearrange("p j r c -> p (j r) c"),
+                    axis=mybir.AxisListType.X,
                     op=ALU.add,
                 )
+
+        def project_plain(i, c, result):
+            for w in range(WEIGHTS):
+                acc = multiply(i, c, w)
+                nc.scalar.copy(out=result[w][:, N_TILE * c : N_TILE * (c + 1)], in_=acc[:])
 
         def tiles_from(first):
             return range(first, min(first + RUN, TOKEN_TILES))
@@ -220,6 +250,7 @@ def tile_wqkv_pa_kernel(
             sort_tile(t)
         for t in tiles_from(0):
             turn_tile(t)
+        make_rotation()
         quantise_tile(0)
         for i in range(TOKEN_TILES):
             if i % RUN == RUN - 1:
@@ -233,8 +264,7 @@ def tile_wqkv_pa_kernel(
             result = [
                 results.tile([P, OUT_COLS], F32, name="result%d" % w) for w in range(WEIGHTS)
             ]
-            project(i, 0, nc.vector.tensor_copy, result)
-            rope(i, result)
-            project(i, 1, nc.scalar.copy, result)
+            project_with_rope(i, result)
+            project_plain(i, 1, result)
             for w in range(WEIGHTS):
                 nc.sync.dma_start(out=out_dram[w][:, i, :], in_=result[w][:])

@@ -49,7 +49,7 @@ def tile_wqkv_pa_kernel(
         ctx.enter_context(tc.manual_schedule())
         keep = ctx.enter_context(tc.tile_pool(name="keep", bufs=1))
         stage = ctx.enter_context(tc.tile_pool(name="stage", bufs=3))
-        results = ctx.enter_context(tc.tile_pool(name="results", bufs=4))
+        results = ctx.enter_context(tc.tile_pool(name="results", bufs=8))
         ordered = ctx.enter_context(tc.tile_pool(name="ordered", bufs=2 * RUN))
         flipped = ctx.enter_context(tc.psum_pool(name="flipped", bufs=RUN))
         sums = ctx.enter_context(tc.psum_pool(name="sums", bufs=6))
@@ -214,34 +214,29 @@ def tile_wqkv_pa_kernel(
                 )
             return acc
 
-        def project_with_rope(i, result):
-            products = []
-            for w in range(WEIGHTS):
-                acc = multiply(i, 0, w)
-                terms = stage.tile([P, ROPE_PAIRS, 2, 2], F32, name="terms%d" % w)
-                nc.vector.tensor_tensor(
-                    out=terms[:],
-                    in0=acc[:, 0:ROPE_COLS]
-                    .rearrange("p (j c) -> p j c", c=2)
-                    .unsqueeze(2)
-                    .to_broadcast([P, ROPE_PAIRS, 2, 2]),
-                    in1=rotation[:, i].rearrange("p j (r c) -> p j r c", c=2),
-                    op=ALU.mult,
-                )
-                nc.vector.tensor_copy(out=result[w][:, ROPE_COLS:N_TILE], in_=acc[:, ROPE_COLS:N_TILE])
-                products.append(terms)
-            for w in range(WEIGHTS):
-                nc.vector.tensor_reduce(
-                    out=result[w][:, 0:ROPE_COLS],
-                    in_=products[w][:].rearrange("p j r c -> p (j r) c"),
-                    axis=mybir.AxisListType.X,
-                    op=ALU.add,
-                )
-
-        def project_plain(i, c, result):
-            for w in range(WEIGHTS):
-                acc = multiply(i, c, w)
-                nc.scalar.copy(out=result[w][:, N_TILE * c : N_TILE * (c + 1)], in_=acc[:])
+        def project(i, w):
+            result = results.tile([P, OUT_COLS], F32, name="result")
+            acc = multiply(i, 0, w)
+            terms = stage.tile([P, ROPE_PAIRS, 2, 2], F32, name="terms")
+            nc.vector.tensor_tensor(
+                out=terms[:],
+                in0=acc[:, 0:ROPE_COLS]
+                .rearrange("p (j c) -> p j c", c=2)
+                .unsqueeze(2)
+                .to_broadcast([P, ROPE_PAIRS, 2, 2]),
+                in1=rotation[:, i].rearrange("p j (r c) -> p j r c", c=2),
+                op=ALU.mult,
+            )
+            nc.vector.tensor_copy(out=result[:, ROPE_COLS:N_TILE], in_=acc[:, ROPE_COLS:N_TILE])
+            nc.vector.tensor_reduce(
+                out=result[:, 0:ROPE_COLS],
+                in_=terms[:].rearrange("p j r c -> p (j r) c"),
+                axis=mybir.AxisListType.X,
+                op=ALU.add,
+            )
+            acc = multiply(i, 1, w)
+            nc.scalar.copy(out=result[:, N_TILE:OUT_COLS], in_=acc[:])
+            nc.sync.dma_start(out=out_dram[w][:, i, :], in_=result[:])
 
         def tiles_from(first):
             return range(first, min(first + RUN, TOKEN_TILES))
@@ -261,10 +256,5 @@ def tile_wqkv_pa_kernel(
             if i % RUN == 0:
                 for t in tiles_from(i + RUN):
                     sort_tile(t)
-            result = [
-                results.tile([P, OUT_COLS], F32, name="result%d" % w) for w in range(WEIGHTS)
-            ]
-            project_with_rope(i, result)
-            project_plain(i, 1, result)
             for w in range(WEIGHTS):
-                nc.sync.dma_start(out=out_dram[w][:, i, :], in_=result[w][:])
+                project(i, w)

@@ -30,6 +30,7 @@ ROPE_PAIRS = ROPE_COLS // 2
 ROPE_BASE = 1e4
 ROUND_TO_INTEGER = 1.5 * 2.0**23
 RUN = 2
+WEIGHT_PIECES = (2, 1)
 
 FLOPS = 2 * TOKENS * CHANNELS * OUT_COLS * WEIGHTS
 
@@ -62,8 +63,14 @@ def tile_wqkv_pa_kernel(
             nc.sync.dma_start(out=x_group[:], in_=x_dram[:, first : first + count, :])
             x_tiles.extend([x_group[:, j, :] for j in range(count)])
 
+        piece_cols = [OUT_COLS // count for count in WEIGHT_PIECES]
         w_words = [
-            keep.tile([P, PASSES, 2 * OUT_COLS], U8, name="w_words%d" % w, align_bytes=64)
+            [
+                keep.tile(
+                    [P, PASSES, 2 * piece_cols[w]], U8, name="w_words%d_%d" % (w, h), align_bytes=64
+                )
+                for h in range(WEIGHT_PIECES[w])
+            ]
             for w in range(WEIGHTS)
         ]
         w_scales = [
@@ -73,11 +80,14 @@ def tile_wqkv_pa_kernel(
         for w in range(WEIGHTS):
             nc.vector.memset(w_scales[w][:].rearrange("p g n -> p (g n)").bitcast(I32), 0)
 
-        def load_weight(w):
+        def load_words(w, h):
+            word_bytes = slice(2 * piece_cols[w] * h, 2 * piece_cols[w] * (h + 1))
             nc.sync.dma_start(
-                out=w_words[w][:].bitcast(I32),
-                in_=words_dram[w].bitcast(I32).rearrange("g p b -> p g b"),
+                out=w_words[w][h][:].bitcast(I32),
+                in_=words_dram[w][:, :, word_bytes].bitcast(I32).rearrange("g p b -> p g b"),
             )
+
+        def load_scales(w):
             for r in range(4):
                 nc.sync.dma_start(
                     out=w_scales[w][r:P:32, :, :].bitcast(I32),
@@ -86,8 +96,11 @@ def tile_wqkv_pa_kernel(
 
         load_x(1)
         load_x(1)
-        load_weight(0)
-        load_weight(1)
+        load_words(0, 0)
+        load_scales(0)
+        load_words(0, 1)
+        load_words(1, 0)
+        load_scales(1)
         while len(x_tiles) < TOKEN_TILES:
             load_x(len(x_tiles))
 
@@ -165,8 +178,40 @@ def tile_wqkv_pa_kernel(
 
         x_sorted = {}
         x_grouped = {}
-        x_codes = {}
-        x_scales = {}
+        x_operand = {}
+
+        def turn_pass(i, g, turned):
+            if i in x_sorted:
+                halves = [x_sorted[i][:, g, u, :] for u in range(2)]
+            else:
+                words = x_tiles[i].bitcast(F32)
+                halves = [
+                    words[:, PASS_WORDS * g + u : PASS_WORDS * (g + 1) : 2] for u in range(2)
+                ]
+            for u in range(2):
+                nc.tensor.transpose(turned[:, u, :], halves[u], identity[:])
+
+        def first_tile():
+            grouped = []
+            for g in range(PASSES):
+                turned = sums.tile([P, 2, P], F32, name="acc")
+                turn_pass(0, g, turned)
+                half = keep.tile([P, P, PACK], BF16, name="first_grouped%d" % g, align_bytes=64)
+                copy_out = nc.vector.tensor_copy if g == 0 else nc.scalar.copy
+                copy_out(out=half[:].bitcast(F32), in_=turned[:].rearrange("p u r -> p r u"))
+                grouped.append(half)
+            return grouped
+
+        def quantise_first_tile(grouped):
+            for g in range(PASSES):
+                codes = keep.tile([P, P], U32, name="first_codes%d" % g, align_bytes=64)
+                scales = keep.tile([P, P], U8, name="first_scales%d" % g, align_bytes=64)
+                nc.vector.quantize_mx(
+                    out=codes[:].bitcast(FP8X4),
+                    scales=scales[:],
+                    in_=grouped[g][:].rearrange("p r t -> p (r t)"),
+                )
+                x_operand[(0, g)] = (codes[:], scales[:])
 
         def sort_tile(i):
             words = ordered.tile([P, PASSES, 2, P], F32, name="words")
@@ -179,8 +224,7 @@ def tile_wqkv_pa_kernel(
         def turn_tile(i):
             turned = flipped.tile([P, PASSES, 2, P], F32, name="turned")
             for g in range(PASSES):
-                for u in range(2):
-                    nc.tensor.transpose(turned[:, g, u, :], x_sorted[i][:, g, u, :], identity[:])
+                turn_pass(i, g, turned[:, g])
             grouped = stage.tile([P, PASSES, P, PACK], BF16, name="grouped", align_bytes=64)
             nc.scalar.copy(
                 out=grouped[:].bitcast(F32), in_=turned[:].rearrange("p g u r -> p g r u")
@@ -195,19 +239,22 @@ def tile_wqkv_pa_kernel(
                 scales=scales[:],
                 in_=x_grouped[i][:].rearrange("p g r t -> p (g r t)"),
             )
-            x_codes[i] = codes
-            x_scales[i] = scales
+            for g in range(PASSES):
+                tokens = slice(P * g, P * (g + 1))
+                x_operand[(i, g)] = (codes[:, tokens], scales[:, tokens])
 
         def multiply(i, c, w):
             first_col = N_TILE * c
+            h = first_col // piece_cols[w]
+            first_byte = 2 * (first_col - piece_cols[w] * h)
             acc = sums.tile([P, N_TILE], F32, name="acc")
             for g in range(PASSES):
-                tokens = slice(P * g, P * (g + 1))
+                codes, scales = x_operand[(i, g)]
                 nc.tensor.matmul_mx(
                     out=acc[:],
-                    lhsT=x_codes[i][:, tokens].bitcast(FP8X4),
-                    lhsT_scale=x_scales[i][:, tokens],
-                    rhs=w_words[w][:, g, 2 * first_col : 2 * (first_col + N_TILE)].bitcast(FP4X4),
+                    lhsT=codes.bitcast(FP8X4),
+                    lhsT_scale=scales,
+                    rhs=w_words[w][h][:, g, first_byte : first_byte + 2 * N_TILE].bitcast(FP4X4),
                     rhs_scale=w_scales[w][:, g, first_col : first_col + N_TILE],
                     start=(g == 0),
                     stop=(g == PASSES - 1),
@@ -238,23 +285,25 @@ def tile_wqkv_pa_kernel(
             nc.scalar.copy(out=result[:, N_TILE:OUT_COLS], in_=acc[:])
             nc.sync.dma_start(out=out_dram[w][:, i, :], in_=result[:])
 
-        def tiles_from(first):
-            return range(first, min(first + RUN, TOKEN_TILES))
-
-        for t in tiles_from(0):
-            sort_tile(t)
-        for t in tiles_from(0):
-            turn_tile(t)
+        first_grouped = first_tile()
+        turn_tile(1)
+        quantise_first_tile(first_grouped)
         make_rotation()
-        quantise_tile(0)
-        for i in range(TOKEN_TILES):
-            if i % RUN == RUN - 1:
-                for t in tiles_from(i + 1):
-                    turn_tile(t)
-            if i + 1 < TOKEN_TILES:
-                quantise_tile(i + 1)
+        quantise_tile(1)
+        project(0, 0)
+        project(1, 0)
+        sort_tile(2)
+        sort_tile(3)
+        project(0, 1)
+        for i in range(1, TOKEN_TILES):
             if i % RUN == 0:
-                for t in tiles_from(i + RUN):
+                quantise_tile(i + 1)
+                for t in range(i + RUN, min(i + 2 * RUN, TOKEN_TILES)):
                     sort_tile(t)
-            for w in range(WEIGHTS):
-                project(i, w)
+            if i > 1:
+                project(i, 0)
+            if i % RUN == 1 and i + 1 < TOKEN_TILES:
+                for t in range(i + 1, i + 1 + RUN):
+                    turn_tile(t)
+                quantise_tile(i + 1)
+            project(i, 1)

@@ -99,10 +99,10 @@ def tile_wqkv_pa_kernel(
         load_words(0, 0)
         load_scales(0)
         load_words(0, 1)
+        load_x(2)
         load_words(1, 0)
         load_scales(1)
-        while len(x_tiles) < TOKEN_TILES:
-            load_x(len(x_tiles))
+        load_x(4)
 
         position = keep.tile([P, TOKEN_TILES], F32, name="position")
         nc.gpsimd.iota(
@@ -290,20 +290,23 @@ def tile_wqkv_pa_kernel(
         quantise_first_tile(first_grouped)
         make_rotation()
         quantise_tile(1)
-        project(0, 0)
-        project(1, 0)
-        sort_tile(2)
-        sort_tile(3)
-        project(0, 1)
-        for i in range(1, TOKEN_TILES):
-            if i % RUN == 0:
-                quantise_tile(i + 1)
-                for t in range(i + RUN, min(i + 2 * RUN, TOKEN_TILES)):
-                    sort_tile(t)
-            if i > 1:
-                project(i, 0)
+        for t in range(RUN, 2 * RUN):
+            sort_tile(t)
+        for i in range(RUN):
+            project(i, 0)
+        for t in range(RUN, 2 * RUN):
+            turn_tile(t)
+        quantise_tile(RUN)
+        for i in range(RUN):
+            project(i, 1)
+        for i in range(RUN, TOKEN_TILES):
             if i % RUN == 1 and i + 1 < TOKEN_TILES:
                 for t in range(i + 1, i + 1 + RUN):
                     turn_tile(t)
+            if i + 1 < TOKEN_TILES:
                 quantise_tile(i + 1)
-            project(i, 1)
+            if i % RUN == 0:
+                for t in range(i + RUN, min(i + 2 * RUN, TOKEN_TILES)):
+                    sort_tile(t)
+            for w in range(WEIGHTS):
+                project(i, w)

@@ -113,43 +113,25 @@ def tile_wqkv_pa_kernel(
             allow_small_or_imprecise_dtypes=True,
         )
         identity = keep.tile([P, P], F32, name="identity")
-        make_identity(nc, identity[:])
+        nc.vector.memset(identity[:], 0.0)
+        make_identity(nc, identity[:], nomemset=True)
 
         warm = keep.tile([P, 1], F32, name="warm")
         nc.scalar.activation(
             out=warm[:], in_=position[:, 0:1], func=mybir.ActivationFunctionType.Sin, scale=0.0
         )
 
-        turns = keep.tile([P, TOKEN_TILES, 2, ROPE_PAIRS], F32, name="turns")
-        nc.gpsimd.tensor_scalar(
-            out=turns[:, :, 1, 0],
-            in0=position[:],
-            scalar1=1.0 / (2.0 * math.pi),
-            scalar2=0.0,
-            op0=ALU.mult,
-            op1=ALU.add,
-        )
-        done = 1
-        while done < ROPE_PAIRS:
-            nc.gpsimd.tensor_scalar(
-                out=turns[:, :, 1, done : 2 * done],
-                in0=turns[:, :, 1, 0:done],
-                scalar1=ROPE_BASE ** (-2.0 * done / ROPE_COLS),
-                scalar2=0.0,
+        turns = keep.tile([P, TOKEN_TILES, ROPE_PAIRS], F32, name="turns")
+        for j in range(ROPE_PAIRS):
+            nc.vector.tensor_scalar(
+                out=turns[:, :, j],
+                in0=position[:],
+                scalar1=1.0 / (2.0 * math.pi * ROPE_BASE ** (2.0 * j / ROPE_COLS)),
+                scalar2=None,
                 op0=ALU.mult,
-                op1=ALU.add,
             )
-            done *= 2
-        nc.gpsimd.tensor_scalar(
-            out=turns[:, :, 0, :],
-            in0=turns[:, :, 1, :],
-            scalar1=1.0,
-            scalar2=0.25,
-            op0=ALU.mult,
-            op1=ALU.add,
-        )
-        whole = keep.tile([P, TOKEN_TILES, 2, ROPE_PAIRS], F32, name="whole")
-        nc.gpsimd.tensor_scalar(
+        whole = keep.tile([P, TOKEN_TILES, ROPE_PAIRS], F32, name="whole")
+        nc.vector.tensor_scalar(
             out=whole[:],
             in0=turns[:],
             scalar1=ROUND_TO_INTEGER,
@@ -157,21 +139,24 @@ def tile_wqkv_pa_kernel(
             op0=ALU.add,
             op1=ALU.subtract,
         )
-        part = keep.tile([P, TOKEN_TILES, 2, ROPE_PAIRS], F32, name="part")
-        nc.gpsimd.tensor_tensor(out=part[:], in0=turns[:], in1=whole[:], op=ALU.subtract)
+        part = keep.tile([P, TOKEN_TILES, ROPE_PAIRS], F32, name="part")
+        nc.vector.tensor_tensor(out=part[:], in0=turns[:], in1=whole[:], op=ALU.subtract)
+        size = keep.tile([P, TOKEN_TILES, ROPE_PAIRS], F32, name="size")
         rotation = keep.tile([P, TOKEN_TILES, ROPE_PAIRS, 4], F32, name="rotation")
 
         def make_rotation():
+            nc.scalar.activation(out=size[:], in_=part[:], func=mybir.ActivationFunctionType.Abs)
             nc.scalar.activation(
                 out=rotation[:, :, :, 0:4:3],
-                in_=part[:, :, 0, :].unsqueeze(3).to_broadcast([P, TOKEN_TILES, ROPE_PAIRS, 2]),
+                in_=size[:].unsqueeze(3).to_broadcast([P, TOKEN_TILES, ROPE_PAIRS, 2]),
                 func=mybir.ActivationFunctionType.Sin,
-                scale=2.0 * math.pi,
+                scale=-2.0 * math.pi,
+                bias=0.5 * math.pi,
             )
             for entry, sign in ((1, -1.0), (2, 1.0)):
                 nc.scalar.activation(
                     out=rotation[:, :, :, entry],
-                    in_=part[:, :, 1, :],
+                    in_=part[:],
                     func=mybir.ActivationFunctionType.Sin,
                     scale=sign * 2.0 * math.pi,
                 )

@@ -30,6 +30,7 @@ ROPE_PAIRS = ROPE_COLS // 2
 ROPE_BASE = 1e4
 ROUND_TO_INTEGER = 1.5 * 2.0**23
 RUN = 2
+IDLE_MATMULS = 2
 WEIGHT_PIECES = (2, 1)
 
 FLOPS = 2 * TOKENS * CHANNELS * OUT_COLS * WEIGHTS
@@ -54,6 +55,12 @@ def tile_wqkv_pa_kernel(
         ordered = ctx.enter_context(tc.tile_pool(name="ordered", bufs=2 * RUN))
         flipped = ctx.enter_context(tc.psum_pool(name="flipped", bufs=RUN))
         sums = ctx.enter_context(tc.psum_pool(name="sums", bufs=6))
+
+        zeros = keep.tile([P, N_TILE], BF16, name="zeros")
+        nc.vector.memset(zeros[:], 0.0)
+        for n in range(IDLE_MATMULS):
+            unread = sums.tile([P, N_TILE], F32, name="acc")
+            nc.tensor.matmul(out=unread[:], lhsT=zeros[:, 0:P], rhs=zeros[:], start=True, stop=True)
 
         x_tiles = []
 

@@ -30,8 +30,8 @@ ROPE_PAIRS = ROPE_COLS // 2
 ROPE_BASE = 1e4
 ROUND_TO_INTEGER = 1.5 * 2.0**23
 RUN = 2
-IDLE_MATMULS = 2
-WEIGHT_PIECES = (2, 1)
+IDLE_MATMULS = 3
+WEIGHT_PIECES = (2, 2)
 
 FLOPS = 2 * TOKENS * CHANNELS * OUT_COLS * WEIGHTS
 
@@ -107,8 +107,9 @@ def tile_wqkv_pa_kernel(
         load_scales(0)
         load_words(0, 1)
         load_x(2)
-        load_words(1, 0)
         load_scales(1)
+        load_words(1, 0)
+        load_words(1, 1)
         load_x(4)
 
         position = keep.tile([P, TOKEN_TILES], F32, name="position")

@@ -31,7 +31,6 @@ ROPE_BASE = 1e4
 ROUND_TO_INTEGER = 1.5 * 2.0**23
 RUN = 2
 IDLE_MATMULS = 3
-WEIGHT_PIECES = (2, 2)
 
 FLOPS = 2 * TOKENS * CHANNELS * OUT_COLS * WEIGHTS
 
@@ -70,13 +69,10 @@ def tile_wqkv_pa_kernel(
             nc.sync.dma_start(out=x_group[:], in_=x_dram[:, first : first + count, :])
             x_tiles.extend([x_group[:, j, :] for j in range(count)])
 
-        piece_cols = [OUT_COLS // count for count in WEIGHT_PIECES]
         w_words = [
             [
-                keep.tile(
-                    [P, PASSES, 2 * piece_cols[w]], U8, name="w_words%d_%d" % (w, h), align_bytes=64
-                )
-                for h in range(WEIGHT_PIECES[w])
+                keep.tile([P, 2 * OUT_COLS], U8, name="w_words%d_%d" % (w, g), align_bytes=64)
+                for g in range(PASSES)
             ]
             for w in range(WEIGHTS)
         ]
@@ -87,12 +83,8 @@ def tile_wqkv_pa_kernel(
         for w in range(WEIGHTS):
             nc.vector.memset(w_scales[w][:].rearrange("p g n -> p (g n)").bitcast(I32), 0)
 
-        def load_words(w, h):
-            word_bytes = slice(2 * piece_cols[w] * h, 2 * piece_cols[w] * (h + 1))
-            nc.sync.dma_start(
-                out=w_words[w][h][:].bitcast(I32),
-                in_=words_dram[w][:, :, word_bytes].bitcast(I32).rearrange("g p b -> p g b"),
-            )
+        def load_words(w, g):
+            nc.sync.dma_start(out=w_words[w][g][:].bitcast(I32), in_=words_dram[w][g].bitcast(I32))
 
         def load_scales(w):
             for r in range(4):
@@ -107,8 +99,8 @@ def tile_wqkv_pa_kernel(
         load_scales(0)
         load_words(0, 1)
         load_x(2)
-        load_scales(1)
         load_words(1, 0)
+        load_scales(1)
         load_words(1, 1)
         load_x(4)
 
@@ -236,27 +228,32 @@ def tile_wqkv_pa_kernel(
                 tokens = slice(P * g, P * (g + 1))
                 x_operand[(i, g)] = (codes[:, tokens], scales[:, tokens])
 
-        def multiply(i, c, w):
-            first_col = N_TILE * c
-            h = first_col // piece_cols[w]
-            first_byte = 2 * (first_col - piece_cols[w] * h)
-            acc = sums.tile([P, N_TILE], F32, name="acc")
-            for g in range(PASSES):
-                codes, scales = x_operand[(i, g)]
-                nc.tensor.matmul_mx(
-                    out=acc[:],
-                    lhsT=codes.bitcast(FP8X4),
-                    lhsT_scale=scales,
-                    rhs=w_words[w][h][:, g, first_byte : first_byte + 2 * N_TILE].bitcast(FP4X4),
-                    rhs_scale=w_scales[w][:, g, first_col : first_col + N_TILE],
-                    start=(g == 0),
-                    stop=(g == PASSES - 1),
-                )
-            return acc
+        def multiply_pass(acc, i, w, c, g):
+            codes, scales = x_operand[(i, g)]
+            nc.tensor.matmul_mx(
+                out=acc[:],
+                lhsT=codes.bitcast(FP8X4),
+                lhsT_scale=scales,
+                rhs=w_words[w][g][:, 2 * N_TILE * c : 2 * N_TILE * (c + 1)].bitcast(FP4X4),
+                rhs_scale=w_scales[w][:, g, N_TILE * c : N_TILE * (c + 1)],
+                start=(g == 0),
+                stop=(g == PASSES - 1),
+            )
+
+        def multiply(i, w):
+            accs = []
+            for c in range(COL_TILES):
+                acc = sums.tile([P, N_TILE], F32, name="acc")
+                accs.append(acc)
+            by_pass = [(c, g) for g in range(PASSES) for c in range(COL_TILES)]
+            by_columns = [(c, g) for c in range(COL_TILES) for g in range(PASSES)]
+            for c, g in by_pass if i == 0 else by_columns:
+                multiply_pass(accs[c], i, w, c, g)
+            return accs
 
         def project(i, w):
             result = results.tile([P, OUT_COLS], F32, name="result")
-            acc = multiply(i, 0, w)
+            acc, second_acc = multiply(i, w)
             terms = stage.tile([P, ROPE_PAIRS, 2, 2], F32, name="terms")
             nc.vector.tensor_tensor(
                 out=terms[:],
@@ -274,8 +271,7 @@ def tile_wqkv_pa_kernel(
                 axis=mybir.AxisListType.X,
                 op=ALU.add,
             )
-            acc = multiply(i, 1, w)
-            nc.scalar.copy(out=result[:, N_TILE:OUT_COLS], in_=acc[:])
+            nc.scalar.copy(out=result[:, N_TILE:OUT_COLS], in_=second_acc[:])
             nc.sync.dma_start(out=out_dram[w][:, i, :], in_=result[:])
 
         first_grouped = first_tile()

@@ -56,7 +56,7 @@ def tile_wqkv_pa_kernel(
         sums = ctx.enter_context(tc.psum_pool(name="sums", bufs=6))
 
         zeros = keep.tile([P, N_TILE], BF16, name="zeros")
-        nc.vector.memset(zeros[:], 0.0)
+        nc.vector.memset(zeros[:].bitcast(I32), 0)
         for n in range(IDLE_MATMULS):
             unread = sums.tile([P, N_TILE], F32, name="acc")
             nc.tensor.matmul(out=unread[:], lhsT=zeros[:, 0:P], rhs=zeros[:], start=True, stop=True)
@@ -80,8 +80,10 @@ def tile_wqkv_pa_kernel(
             keep.tile([P, PASSES, OUT_COLS], U8, name="w_scales%d" % w, align_bytes=64)
             for w in range(WEIGHTS)
         ]
-        for w in range(WEIGHTS):
-            nc.vector.memset(w_scales[w][:].rearrange("p g n -> p (g n)").bitcast(I32), 0)
+        identity = keep.tile([P, P], F32, name="identity")
+        nc.vector.memset(w_scales[0][:].rearrange("p g n -> p (g n)").bitcast(I32), 0)
+        nc.vector.memset(identity[:], 0.0)
+        nc.vector.memset(w_scales[1][:].rearrange("p g n -> p (g n)").bitcast(I32), 0)
 
         def load_words(w, g):
             nc.sync.dma_start(out=w_words[w][g][:].bitcast(I32), in_=words_dram[w][g].bitcast(I32))
@@ -112,8 +114,6 @@ def tile_wqkv_pa_kernel(
             channel_multiplier=TOKEN_TILES,
             allow_small_or_imprecise_dtypes=True,
         )
-        identity = keep.tile([P, P], F32, name="identity")
-        nc.vector.memset(identity[:], 0.0)
         make_identity(nc, identity[:], nomemset=True)
 
         warm = keep.tile([P, 1], F32, name="warm")
@@ -182,8 +182,7 @@ def tile_wqkv_pa_kernel(
                 turned = sums.tile([P, 2, P], F32, name="acc")
                 turn_pass(0, g, turned)
                 half = keep.tile([P, P, PACK], BF16, name="first_grouped%d" % g, align_bytes=64)
-                copy_out = nc.vector.tensor_copy if g == 0 else nc.scalar.copy
-                copy_out(out=half[:].bitcast(F32), in_=turned[:].rearrange("p u r -> p r u"))
+                nc.scalar.copy(out=half[:].bitcast(F32), in_=turned[:].rearrange("p u r -> p r u"))
                 grouped.append(half)
             return grouped
 

import math
from contextlib import ExitStack

import concourse.mybir as mybir
from concourse.masks import make_identity

F32 = mybir.dt.float32
BF16 = mybir.dt.bfloat16
I32 = mybir.dt.int32
U32 = mybir.dt.uint32
U8 = mybir.dt.uint8
FP8X4 = mybir.dt.float8_e4m3fn_x4
FP4X4 = mybir.dt.float4_e2m1fn_x4
ALU = mybir.AluOpType

P = 128
PACK = 4
K_PASS = P * PACK
PASS_WORDS = K_PASS // 2
TOKENS = 1024
CHANNELS = 1024
OUT_COLS = 1024
PASSES = CHANNELS // K_PASS
TOKEN_TILES = TOKENS // P
N_TILE = 512
COL_TILES = OUT_COLS // N_TILE
WEIGHTS = 2
ROPE_COLS = 16
ROPE_PAIRS = ROPE_COLS // 2
ROPE_BASE = 1e4
ROUND_TO_INTEGER = 1.5 * 2.0**23
RUN = 2
IDLE_MATMULS = 3

FLOPS = 2 * TOKENS * CHANNELS * OUT_COLS * WEIGHTS


def tile_wqkv_pa_kernel(
    tc, Q_in, W_Q_words, W_Q_scales, W_K_words, W_K_scales, out_0, out_1
):
    nc = tc.nc
    x_dram = Q_in.rearrange("b (p i) c -> (b p) i c", i=TOKEN_TILES)
    out_dram = [
        out.rearrange("b (p i) e -> (b p) i e", i=TOKEN_TILES) for out in (out_0, out_1)
    ]
    words_dram = [W_Q_words, W_K_words]
    scales_dram = [W_Q_scales, W_K_scales]

    with ExitStack() as ctx:
        ctx.enter_context(tc.manual_schedule())
        keep = ctx.enter_context(tc.tile_pool(name="keep", bufs=1))
        stage = ctx.enter_context(tc.tile_pool(name="stage", bufs=3))
        results = ctx.enter_context(tc.tile_pool(name="results", bufs=8))
        ordered = ctx.enter_context(tc.tile_pool(name="ordered", bufs=2 * RUN))
        flipped = ctx.enter_context(tc.psum_pool(name="flipped", bufs=RUN))
        sums = ctx.enter_context(tc.psum_pool(name="sums", bufs=6))

        zeros = keep.tile([P, N_TILE], BF16, name="zeros")
        nc.vector.memset(zeros[:].bitcast(I32), 0)
        for n in range(IDLE_MATMULS):
            unread = sums.tile([P, N_TILE], F32, name="acc")
            nc.tensor.matmul(out=unread[:], lhsT=zeros[:, 0:P], rhs=zeros[:], start=True, stop=True)

        x_tiles = []

        def load_x(count):
            first = len(x_tiles)
            x_group = keep.tile([P, count, CHANNELS], BF16, name="x%d" % first)
            nc.sync.dma_start(out=x_group[:], in_=x_dram[:, first : first + count, :])
            x_tiles.extend([x_group[:, j, :] for j in range(count)])

        w_words = [
            [
                keep.tile([P, 2 * OUT_COLS], U8, name="w_words%d_%d" % (w, g), align_bytes=64)
                for g in range(PASSES)
            ]
            for w in range(WEIGHTS)
        ]
        w_scales = [
            keep.tile([P, PASSES, OUT_COLS], U8, name="w_scales%d" % w, align_bytes=64)
            for w in range(WEIGHTS)
        ]
        identity = keep.tile([P, P], F32, name="identity")
        nc.vector.memset(w_scales[0][:].rearrange("p g n -> p (g n)").bitcast(I32), 0)
        nc.vector.memset(identity[:], 0.0)
        nc.vector.memset(w_scales[1][:].rearrange("p g n -> p (g n)").bitcast(I32), 0)

        def load_words(w, g):
            nc.sync.dma_start(out=w_words[w][g][:].bitcast(I32), in_=words_dram[w][g].bitcast(I32))

        def load_scales(w):
            for r in range(4):
                nc.sync.dma_start(
                    out=w_scales[w][r:P:32, :, :].bitcast(I32),
                    in_=scales_dram[w].bitcast(I32)[:, r:16:4, :].rearrange("g q n -> q g n"),
                )

        load_x(1)
        load_x(1)
        load_words(0, 0)
        load_scales(0)
        load_words(0, 1)
        load_x(2)
        load_words(1, 0)
        load_scales(1)
        load_words(1, 1)
        load_x(4)

        position = keep.tile([P, TOKEN_TILES], F32, name="position")
        nc.gpsimd.iota(
            position[:],
            pattern=[[1, TOKEN_TILES]],
            base=0,
            channel_multiplier=TOKEN_TILES,
            allow_small_or_imprecise_dtypes=True,
        )
        make_identity(nc, identity[:], nomemset=True)

        warm = keep.tile([P, 1], F32, name="warm")
        nc.scalar.activation(
            out=warm[:], in_=position[:, 0:1], func=mybir.ActivationFunctionType.Sin, scale=0.0
        )

        turns = keep.tile([P, TOKEN_TILES, ROPE_PAIRS], F32, name="turns")
        for j in range(ROPE_PAIRS):
            nc.vector.tensor_scalar(
                out=turns[:, :, j],
                in0=position[:],
                scalar1=1.0 / (2.0 * math.pi * ROPE_BASE ** (2.0 * j / ROPE_COLS)),
                scalar2=None,
                op0=ALU.mult,
            )
        whole = keep.tile([P, TOKEN_TILES, ROPE_PAIRS], F32, name="whole")
        nc.vector.tensor_scalar(
            out=whole[:],
            in0=turns[:],
            scalar1=ROUND_TO_INTEGER,
            scalar2=ROUND_TO_INTEGER,
            op0=ALU.add,
            op1=ALU.subtract,
        )
        part = keep.tile([P, TOKEN_TILES, ROPE_PAIRS], F32, name="part")
        nc.vector.tensor_tensor(out=part[:], in0=turns[:], in1=whole[:], op=ALU.subtract)
        size = keep.tile([P, TOKEN_TILES, ROPE_PAIRS], F32, name="size")
        rotation = keep.tile([P, TOKEN_TILES, ROPE_PAIRS, 4], F32, name="rotation")

        def make_rotation():
            nc.scalar.activation(out=size[:], in_=part[:], func=mybir.ActivationFunctionType.Abs)
            nc.scalar.activation(
                out=rotation[:, :, :, 0:4:3],
                in_=size[:].unsqueeze(3).to_broadcast([P, TOKEN_TILES, ROPE_PAIRS, 2]),
                func=mybir.ActivationFunctionType.Sin,
                scale=-2.0 * math.pi,
                bias=0.5 * math.pi,
            )
            for entry, sign in ((1, -1.0), (2, 1.0)):
                nc.scalar.activation(
                    out=rotation[:, :, :, entry],
                    in_=part[:],
                    func=mybir.ActivationFunctionType.Sin,
                    scale=sign * 2.0 * math.pi,
                )

        x_sorted = {}
        x_grouped = {}
        x_operand = {}

        def turn_pass(i, g, turned):
            if i in x_sorted:
                halves = [x_sorted[i][:, g, u, :] for u in range(2)]
            else:
                words = x_tiles[i].bitcast(F32)
                halves = [
                    words[:, PASS_WORDS * g + u : PASS_WORDS * (g + 1) : 2] for u in range(2)
                ]
            for u in range(2):
                nc.tensor.transpose(turned[:, u, :], halves[u], identity[:])

        def first_tile():
            grouped = []
            for g in range(PASSES):
                turned = sums.tile([P, 2, P], F32, name="acc")
                turn_pass(0, g, turned)
                half = keep.tile([P, P, PACK], BF16, name="first_grouped%d" % g, align_bytes=64)
                nc.scalar.copy(out=half[:].bitcast(F32), in_=turned[:].rearrange("p u r -> p r u"))
                grouped.append(half)
            return grouped

        def quantise_first_tile(grouped):
            for g in range(PASSES):
                codes = keep.tile([P, P], U32, name="first_codes%d" % g, align_bytes=64)
                scales = keep.tile([P, P], U8, name="first_scales%d" % g, align_bytes=64)
                nc.vector.quantize_mx(
                    out=codes[:].bitcast(FP8X4),
                    scales=scales[:],
                    in_=grouped[g][:].rearrange("p r t -> p (r t)"),
                )
                x_operand[(0, g)] = (codes[:], scales[:])

        def sort_tile(i):
            words = ordered.tile([P, PASSES, 2, P], F32, name="words")
            nc.vector.tensor_copy(
                out=words[:],
                in_=x_tiles[i].bitcast(F32).rearrange("p (g q u) -> p g u q", g=PASSES, u=2),
            )
            x_sorted[i] = words

        def turn_tile(i):
            turned = flipped.tile([P, PASSES, 2, P], F32, name="turned")
            for g in range(PASSES):
                turn_pass(i, g, turned[:, g])
            grouped = stage.tile([P, PASSES, P, PACK], BF16, name="grouped", align_bytes=64)
            nc.scalar.copy(
                out=grouped[:].bitcast(F32), in_=turned[:].rearrange("p g u r -> p g r u")
            )
            x_grouped[i] = grouped

        def quantise_tile(i):
            codes = stage.tile([P, PASSES * P], U32, name="codes", align_bytes=64)
            scales = stage.tile([P, PASSES * P], U8, name="scales", align_bytes=64)
            nc.vector.quantize_mx(
                out=codes[:].bitcast(FP8X4),
                scales=scales[:],
                in_=x_grouped[i][:].rearrange("p g r t -> p (g r t)"),
            )
            for g in range(PASSES):
                tokens = slice(P * g, P * (g + 1))
                x_operand[(i, g)] = (codes[:, tokens], scales[:, tokens])

        def multiply_pass(acc, i, w, c, g):
            codes, scales = x_operand[(i, g)]
            nc.tensor.matmul_mx(
                out=acc[:],
                lhsT=codes.bitcast(FP8X4),
                lhsT_scale=scales,
                rhs=w_words[w][g][:, 2 * N_TILE * c : 2 * N_TILE * (c + 1)].bitcast(FP4X4),
                rhs_scale=w_scales[w][:, g, N_TILE * c : N_TILE * (c + 1)],
                start=(g == 0),
                stop=(g == PASSES - 1),
            )

        def multiply(i, w):
            accs = []
            for c in range(COL_TILES):
                acc = sums.tile([P, N_TILE], F32, name="acc")
                accs.append(acc)
            by_pass = [(c, g) for g in range(PASSES) for c in range(COL_TILES)]
            by_columns = [(c, g) for c in range(COL_TILES) for g in range(PASSES)]
            for c, g in by_pass if i == 0 else by_columns:
                multiply_pass(accs[c], i, w, c, g)
            return accs

        def project(i, w):
            result = results.tile([P, OUT_COLS], F32, name="result")
            acc, second_acc = multiply(i, w)
            terms = stage.tile([P, ROPE_PAIRS, 2, 2], F32, name="terms")
            nc.vector.tensor_tensor(
                out=terms[:],
                in0=acc[:, 0:ROPE_COLS]
                .rearrange("p (j c) -> p j c", c=2)
                .unsqueeze(2)
                .to_broadcast([P, ROPE_PAIRS, 2, 2]),
                in1=rotation[:, i].rearrange("p j (r c) -> p j r c", c=2),
                op=ALU.mult,
            )
            nc.vector.tensor_copy(out=result[:, ROPE_COLS:N_TILE], in_=acc[:, ROPE_COLS:N_TILE])
            nc.vector.tensor_reduce(
                out=result[:, 0:ROPE_COLS],
                in_=terms[:].rearrange("p j r c -> p (j r) c"),
                axis=mybir.AxisListType.X,
                op=ALU.add,
            )
            nc.scalar.copy(out=result[:, N_TILE:OUT_COLS], in_=second_acc[:])
            nc.sync.dma_start(out=out_dram[w][:, i, :], in_=result[:])

        first_grouped = first_tile()
        turn_tile(1)
        quantise_first_tile(first_grouped)
        make_rotation()
        quantise_tile(1)
        for t in range(RUN, 2 * RUN):
            sort_tile(t)
        for i in range(RUN):
            project(i, 0)
        for t in range(RUN, 2 * RUN):
            turn_tile(t)
        quantise_tile(RUN)
        for i in range(RUN):
            project(i, 1)
        for i in range(RUN, TOKEN_TILES):
            if i % RUN == 1 and i + 1 < TOKEN_TILES:
                for t in range(i + 1, i + 1 + RUN):
                    turn_tile(t)
            if i + 1 < TOKEN_TILES:
                quantise_tile(i + 1)
            if i % RUN == 0:
                for t in range(i + RUN, min(i + 2 * RUN, TOKEN_TILES)):
                    sort_tile(t)
            for w in range(WEIGHTS):
                project(i, w)
